import numpy as np
import ml_dtypes


def mxq(x, axis, fmt="e4m3"):
    dtype, down = {"e4m3": (ml_dtypes.float8_e4m3fn, 7), "e5m2": (ml_dtypes.float8_e5m2, 14)}[fmt]
    v = np.moveaxis(np.asarray(x, np.float32).astype(ml_dtypes.bfloat16).astype(np.float64), axis, -1)
    blocks = v.reshape(v.shape[:-1] + (-1, 32))
    amax = np.abs(blocks).max(-1, keepdims=True)
    byte = np.maximum(np.where(amax > 0, np.frexp(amax)[1] - 1 + 127, 0) - down, 1)
    scale = np.exp2(byte - 127.0)
    codes = (blocks / scale).astype(np.float32).astype(dtype).astype(np.float64)
    return np.moveaxis((codes * scale).reshape(v.shape), -1, axis)


WIDE = False


def mx_kscale(k):
    if not WIDE:
        return np.ones(k)
    levels = np.array([10, -10, 5, -5, 0])
    a = np.random.permutation(np.resize(levels, k // 512 * 4)).reshape(k // 512, 4)
    idx = np.arange(k)
    return np.exp2(a[idx // 512, idx % 128 // 32])


BF16 = ml_dtypes.bfloat16


def bf(x):
    return np.asarray(x, np.float32).astype(BF16)


def f64(x):
    return np.asarray(x).astype(np.float64)


B, T, D, H, DH, F = 4, 1024, 512, 16, 64, 256
A = H * DH
EPS = 1e-6


def layer_norm(v, gain, bias):
    mu = v.mean(-1, keepdims=True)
    var = np.square(v - mu).mean(-1, keepdims=True)
    return (v - mu) * (1.0 / np.sqrt(var + EPS)) * gain + bias


def gelu_tanh(v):
    return 0.5 * v * (1.0 + np.tanh(np.sqrt(2.0 / np.pi) * (v + 0.044715 * v**3)))


def setup_inputs():
    s, t = mx_kscale(A), mx_kscale(D)
    r = np.random.standard_normal
    return {"attn_out": bf(r((B, T, A)) * 0.3 * s),
            "residual": bf(r((B, T, D))),
            "wo": bf(r((A, D)) * 2.0 / np.sqrt(A) / s[:, None]),
            "bo": bf(0.1 * r(D)),
            "ln2_gain": bf((1.0 + 0.1 * r(D)) * t),
            "ln2_bias": bf(0.1 * r(D) * t),
            "w1": bf(r((D, F)) / np.sqrt(D) / t[:, None]),
            "b1": bf(0.1 * r(F))}


def reference(attn_out, residual, wo, bo, ln2_gain, ln2_bias, w1, b1):
    x_mid = (mxq(f64(attn_out), 2, "e4m3") @ mxq(f64(wo), 0, "e4m3")) + f64(bo) + f64(residual)
    h = layer_norm(x_mid, f64(ln2_gain), f64(ln2_bias))
    g = gelu_tanh((mxq(h, 2, "e4m3") @ mxq(f64(w1), 0, "e4m3")) + f64(b1))
    return x_mid, g

@@ -1,0 +1,329 @@
+from contextlib import ExitStack
+
+import concourse.mybir as mybir
+from concourse.masks import make_identity
+
+F32 = mybir.dt.float32
+BF16 = mybir.dt.bfloat16
+U32 = mybir.dt.uint32
+U8 = mybir.dt.uint8
+FP8X4 = mybir.dt.float8_e4m3fn_x4
+ALU = mybir.AluOpType
+ACT = mybir.ActivationFunctionType
+
+P = 128
+PACK = 4
+K_PASS = P * PACK
+TOKENS = 4 * 1024
+A = 1024
+D = 512
+F = 256
+EPS = 1e-6
+PASSES = A // K_PASS
+CHUNK_TILES = 4
+UNIT_TILES = 2
+UNIT_TOKENS = UNIT_TILES * P
+UNITS = TOKENS // UNIT_TOKENS
+UNITS_PER_CHUNK = CHUNK_TILES // UNIT_TILES
+CHUNKS = UNITS // UNITS_PER_CHUNK
+CHUNK_BUFS = 3
+
+FLOPS = 2 * TOKENS * A * D + 2 * TOKENS * D * F
+
+
+def tile_swidtblock_pb_t_kernel(
+    tc, attn_out, residual, wo, bo, ln2_gain, ln2_bias, w1, b1, out_0, out_1
+):
+    nc = tc.nc
+    attn_chunks = attn_out.flatten_outer_dims().rearrange("(c p i) k -> c p (i k)", p=P, i=CHUNK_TILES)
+    res_chunks = residual.flatten_outer_dims().rearrange("(c p i) d -> c p i d", p=P, i=CHUNK_TILES)
+    x_chunks = out_0.flatten_outer_dims().rearrange("(c p i) d -> c p i d", p=P, i=CHUNK_TILES)
+    g_chunks = out_1.flatten_outer_dims().rearrange("(c p i) f -> c p i f", p=P, i=CHUNK_TILES)
+
+    with ExitStack() as ctx:
+        const = ctx.enter_context(tc.tile_pool(name="const", bufs=1))
+        chunks = ctx.enter_context(tc.tile_pool(name="chunks", bufs=CHUNK_BUFS))
+        work = ctx.enter_context(tc.tile_pool(name="work", bufs=2))
+        held = ctx.enter_context(tc.tile_pool(name="held", bufs=3))
+        psum = ctx.enter_context(tc.psum_pool(name="psum", bufs=2))
+
+        attn_of = {}
+        res_of = {}
+
+        def load_chunk(c):
+            attn_sb = chunks.tile([P, CHUNK_TILES * A], BF16)
+            nc.sync.dma_start(out=attn_sb[:], in_=attn_chunks[c])
+            res_sb = chunks.tile([P, CHUNK_TILES, D], BF16)
+            nc.sync.dma_start(out=res_sb[:], in_=res_chunks[c])
+            attn_of[c] = attn_sb[:].bitcast(F32)
+            res_of[c] = res_sb
+
+        wo_raw = const.tile([P, PASSES, PACK, D], BF16)
+        wo_rows = wo.rearrange("(s u p e) c -> s p u (e c)", s=PASSES, u=2, p=P, e=2)
+        nc.sync.dma_start(out=wo_raw[:, 0].rearrange("p (u e) c -> p u (e c)", e=2), in_=wo_rows[0])
+        load_chunk(0)
+        nc.sync.dma_start(out=wo_raw[:, 1].rearrange("p (u e) c -> p u (e c)", e=2), in_=wo_rows[1])
+        load_chunk(1)
+        load_chunk(2)
+
+        bias_rows = const.tile([P, D + F], BF16)
+        nc.vector.memset(bias_rows[:], 0.0)
+        nc.scalar.dma_start(out=bias_rows[0:1, 0:D], in_=bo.rearrange("(o d) -> o d", o=1))
+        nc.scalar.dma_start(out=bias_rows[0:1, D : D + F], in_=b1.rearrange("(o f) -> o f", o=1))
+        norm_rows = const.tile([P, P], BF16)
+        nc.vector.memset(norm_rows[:], 0.0)
+        nc.scalar.dma_start(out=norm_rows[0:PACK, :], in_=ln2_gain.rearrange("(t p) -> t p", p=P))
+        nc.scalar.dma_start(out=norm_rows[PACK : 2 * PACK, :], in_=ln2_bias.rearrange("(t p) -> t p", p=P))
+        w1_raw = const.tile([P, PACK, F], BF16)
+        nc.scalar.dma_start(out=w1_raw[:], in_=w1.rearrange("(t p) f -> p t f", p=P))
+
+        ident_f32 = const.tile([P, P], F32)
+        make_identity(nc, ident_f32[:])
+        ident_bf16 = const.tile([P, P], BF16)
+        make_identity(nc, ident_bf16[:])
+        ones = const.tile([P, P], BF16)
+        nc.vector.memset(ones[:], 1.0)
+        minus_half = const.tile([P, UNIT_TILES], F32)
+        nc.vector.memset(minus_half[:], -0.5)
+
+        wo_grouped = const.tile([P, PASSES, D * PACK], BF16, align_bytes=64)
+        wo_codes = const.tile([P, PASSES, D], U32, align_bytes=64)
+        wo_scales = const.tile([P, PASSES, D], U8, align_bytes=64)
+        for s in range(PASSES):
+            nc.vector.tensor_copy(
+                out=wo_grouped[:, s, :].rearrange("p (c t) -> p c t", t=PACK),
+                in_=wo_raw[:, s].rearrange("p t c -> p c t"),
+            )
+        for s in range(PASSES):
+            nc.vector.quantize_mx(
+                out=wo_codes[:, s, :].bitcast(FP8X4), scales=wo_scales[:, s, :], in_=wo_grouped[:, s, :]
+            )
+        w1_grouped = const.tile([P, F * PACK], BF16, align_bytes=64)
+        w1_codes = const.tile([P, F], U32, align_bytes=64)
+        w1_scales = const.tile([P, F], U8, align_bytes=64)
+        nc.scalar.copy(
+            out=w1_grouped[:].rearrange("p (f t) -> p f t", t=PACK), in_=w1_raw[:].rearrange("p t f -> p f t")
+        )
+        nc.vector.quantize_mx(out=w1_codes[:].bitcast(FP8X4), scales=w1_scales[:], in_=w1_grouped[:])
+
+        bo_ps = psum.tile([P, D], F32, tag="acc")
+        nc.tensor.matmul(out=bo_ps[:], lhsT=ones[:], rhs=bias_rows[:, 0:D], start=True, stop=True)
+        bo_all = const.tile([P, D], F32)
+        nc.scalar.copy(out=bo_all[:], in_=bo_ps[:])
+        b1_ps = psum.tile([P, F], F32, tag="acc")
+        nc.tensor.matmul(out=b1_ps[:], lhsT=ones[:], rhs=bias_rows[:, D : D + F], start=True, stop=True)
+        b1_all = const.tile([P, F], F32)
+        nc.scalar.copy(out=b1_all[:], in_=b1_ps[:])
+        norm_ps = psum.tile([P, P], BF16, tag="at")
+        nc.tensor.transpose(norm_ps[:], norm_rows[:], ident_bf16[:])
+        norm_cols = const.tile([P, 2 * PACK], F32)
+        nc.scalar.copy(out=norm_cols[:], in_=norm_ps[:, 0 : 2 * PACK])
+
+        live = {}
+
+        def chunk_and_first_tile(u):
+            return u // UNITS_PER_CHUNK, (u % UNITS_PER_CHUNK) * UNIT_TILES
+
+        def transpose_attn(u):
+            c, first = chunk_and_first_tile(u)
+            for i in range(UNIT_TILES):
+                at = psum.tile([P, PASSES * 2, P], F32, tag="at")
+                for w in range(PASSES * 2):
+                    start = (first + i) * (A // 2) + w * P
+                    nc.tensor.transpose(at[:, w, :], attn_of[c][:, start : start + P], ident_f32[:])
+                live["at", u, i] = at
+
+        def group_attn(u):
+            a_grouped = work.tile([P, UNIT_TILES * PASSES * P * PACK], BF16, align_bytes=64)
+            words = a_grouped[:].bitcast(F32).rearrange(
+                "p (i s j u) -> p i s j u", i=UNIT_TILES, s=PASSES, u=2
+            )
+            for i in range(UNIT_TILES):
+                nc.scalar.copy(
+                    out=words[:, i], in_=live["at", u, i][:].rearrange("p (s u) j -> p s j u", u=2)
+                )
+            live["a_grouped", u] = a_grouped
+
+        def quantise_attn(u):
+            a_codes = work.tile([P, UNIT_TILES, PASSES, P], U32, align_bytes=64)
+            a_scales = work.tile([P, UNIT_TILES, PASSES, P], U8, align_bytes=64)
+            nc.vector.quantize_mx(
+                out=a_codes[:].rearrange("p i s j -> p (i s j)").bitcast(FP8X4),
+                scales=a_scales[:].rearrange("p i s j -> p (i s j)"),
+                in_=live["a_grouped", u][:],
+            )
+            live["a_codes", u] = a_codes
+            live["a_scales", u] = a_scales
+
+        def project(u):
+            for i in range(UNIT_TILES):
+                acc = psum.tile([P, D], F32, tag="acc")
+                for s in range(PASSES):
+                    nc.tensor.matmul_mx(
+                        out=acc[:],
+                        lhsT=live["a_codes", u][:, i, s, :].bitcast(FP8X4),
+                        lhsT_scale=live["a_scales", u][:, i, s, :],
+                        rhs=wo_codes[:, s, :].bitcast(FP8X4),
+                        rhs_scale=wo_scales[:, s, :],
+                        start=(s == 0),
+                        stop=(s == PASSES - 1),
+                    )
+                live["acc", u, i] = acc
+
+        def add_bias_to_residual(u):
+            c, first = chunk_and_first_tile(u)
+            res_bo = held.tile([P, UNIT_TILES, D], F32)
+            nc.vector.tensor_tensor(
+                out=res_bo[:],
+                in0=res_of[c][:, first : first + UNIT_TILES, :],
+                in1=bo_all[:].unsqueeze(1).to_broadcast([P, UNIT_TILES, D]),
+                op=ALU.add,
+            )
+            live["res_bo", u] = res_bo
+
+        def finish_x_mid(u):
+            c, first = chunk_and_first_tile(u)
+            x_mid = held.tile([P, UNIT_TILES, D], F32)
+            row_sum = held.tile([P, UNIT_TILES], F32)
+            for i in range(UNIT_TILES):
+                nc.vector.scalar_tensor_tensor(
+                    out=x_mid[:, i, :],
+                    in0=live["acc", u, i][:],
+                    scalar=0.0,
+                    in1=live["res_bo", u][:, i, :],
+                    op0=ALU.add,
+                    op1=ALU.add,
+                    accum_out=row_sum[:, i : i + 1],
+                )
+            nc.sync.dma_start(out=x_chunks[c][:, first : first + UNIT_TILES, :], in_=x_mid[:])
+            live["x_mid", u] = x_mid
+            live["row_sum", u] = row_sum
+
+        def statistics(u):
+            neg_mean = held.tile([P, UNIT_TILES], F32)
+            nc.scalar.mul(out=neg_mean[:], in_=live["row_sum", u][:], mul=-1.0 / D)
+            sq_sum = held.tile([P, UNIT_TILES], F32)
+            for i in range(UNIT_TILES):
+                squares = work.tile([P, D], BF16)
+                nc.scalar.activation(
+                    out=squares[:],
+                    in_=live["x_mid", u][:, i, :],
+                    func=ACT.Square,
+                    bias=neg_mean[:, i : i + 1],
+                    scale=1.0,
+                    accum_out=sq_sum[:, i : i + 1],
+                )
+            var_eps = held.tile([P, UNIT_TILES], F32)
+            nc.gpsimd.tensor_scalar(
+                out=var_eps[:], in0=sq_sum[:], scalar1=1.0 / D, scalar2=EPS, op0=ALU.mult, op1=ALU.add
+            )
+            rstd = held.tile([P, UNIT_TILES], F32)
+            nc.gpsimd.tensor_tensor(out=rstd[:], in0=var_eps[:], in1=minus_half[:], op=ALU.pow)
+            live["neg_mean", u] = neg_mean
+            live["rstd", u] = rstd
+
+        def normalise(u):
+            normed = work.tile([P, UNIT_TILES, D], F32)
+            for i in range(UNIT_TILES):
+                nc.vector.tensor_scalar(
+                    out=normed[:, i, :],
+                    in0=live["x_mid", u][:, i, :],
+                    scalar1=live["neg_mean", u][:, i : i + 1],
+                    scalar2=live["rstd", u][:, i : i + 1],
+                    op0=ALU.add,
+                    op1=ALU.mult,
+                )
+            live["normed", u] = normed
+
+        def transpose_normed(u):
+            for half in range(2):
+                planes = psum.tile([P, PACK // 2, UNIT_TILES, P], F32, tag="planes")
+                for t2 in range(PACK // 2):
+                    t = half * (PACK // 2) + t2
+                    for i in range(UNIT_TILES):
+                        nc.tensor.transpose(
+                            planes[:, t2, i, :], live["normed", u][:, i, t * P : (t + 1) * P], ident_f32[:]
+                        )
+                live["planes", u, half] = planes
+
+        def gain_and_bias(u):
+            h_planes = work.tile([P, PACK, UNIT_TOKENS], BF16)
+            for t in range(PACK):
+                nc.scalar.activation(
+                    out=h_planes[:, t, :],
+                    in_=live["planes", u, t // (PACK // 2)][:, t % (PACK // 2)].rearrange("p i j -> p (i j)"),
+                    func=ACT.Identity,
+                    scale=norm_cols[:, t : t + 1],
+                    bias=norm_cols[:, PACK + t : PACK + t + 1],
+                )
+            live["h_planes", u] = h_planes
+
+        def group_h(u):
+            h_grouped = work.tile([P, UNIT_TOKENS * PACK], BF16, align_bytes=64)
+            nc.vector.tensor_copy(
+                out=h_grouped[:].rearrange("p (j t) -> p j t", t=PACK),
+                in_=live["h_planes", u][:].rearrange("p t j -> p j t"),
+            )
+            live["h_grouped", u] = h_grouped
+
+        def quantise_h(u):
+            h_codes = work.tile([P, UNIT_TOKENS], U32, align_bytes=64)
+            h_scales = work.tile([P, UNIT_TOKENS], U8, align_bytes=64)
+            nc.vector.quantize_mx(out=h_codes[:].bitcast(FP8X4), scales=h_scales[:], in_=live["h_grouped", u][:])
+            live["h_codes", u] = h_codes
+            live["h_scales", u] = h_scales
+
+        def expand(u):
+            acc2 = psum.tile([P, UNIT_TILES, F], F32, tag="acc2")
+            for i in range(UNIT_TILES):
+                nc.tensor.matmul_mx(
+                    out=acc2[:, i, :],
+                    lhsT=live["h_codes", u][:, i * P : (i + 1) * P].bitcast(FP8X4),
+                    lhsT_scale=live["h_scales", u][:, i * P : (i + 1) * P],
+                    rhs=w1_codes[:].bitcast(FP8X4),
+                    rhs_scale=w1_scales[:],
+                    start=True,
+                    stop=True,
+                )
+            live["acc2", u] = acc2
+
+        def add_b1(u):
+            pre_gelu = work.tile([P, UNIT_TILES, F], F32)
+            nc.vector.tensor_tensor(
+                out=pre_gelu[:],
+                in0=live["acc2", u][:],
+                in1=b1_all[:].unsqueeze(1).to_broadcast([P, UNIT_TILES, F]),
+                op=ALU.add,
+            )
+            live["pre_gelu", u] = pre_gelu
+
+        def gelu_and_store(u):
+            c, first = chunk_and_first_tile(u)
+            g_sb = held.tile([P, UNIT_TILES, F], F32)
+            nc.scalar.activation(out=g_sb[:], in_=live["pre_gelu", u][:], func=ACT.Gelu_apprx_tanh)
+            nc.sync.dma_start(out=g_chunks[c][:, first : first + UNIT_TILES, :], in_=g_sb[:])
+
+        def when_valid(stage, u):
+            if 0 <= u < UNITS:
+                stage(u)
+
+        for slot in range(-2, UNITS + 2):
+            if slot % UNITS_PER_CHUNK == 0:
+                next_chunk = slot // UNITS_PER_CHUNK + CHUNK_BUFS
+                if CHUNK_BUFS <= next_chunk < CHUNKS:
+                    load_chunk(next_chunk)
+            when_valid(transpose_normed, slot - 1)
+            when_valid(transpose_attn, slot + 2)
+            when_valid(finish_x_mid, slot)
+            when_valid(gain_and_bias, slot - 1)
+            when_valid(quantise_attn, slot + 1)
+            when_valid(project, slot + 1)
+            when_valid(statistics, slot)
+            when_valid(group_h, slot - 1)
+            when_valid(add_bias_to_residual, slot + 2)
+            when_valid(quantise_h, slot - 1)
+            when_valid(expand, slot - 1)
+            when_valid(gelu_and_store, slot - 2)
+            when_valid(group_attn, slot + 2)
+            when_valid(normalise, slot)
+            when_valid(add_b1, slot - 1)

@@ -20,13 +20,11 @@ D = 512
 F = 256
 EPS = 1e-6
 PASSES = A // K_PASS
-CHUNK_TILES = 4
 UNIT_TILES = 2
 UNIT_TOKENS = UNIT_TILES * P
 UNITS = TOKENS // UNIT_TOKENS
-UNITS_PER_CHUNK = CHUNK_TILES // UNIT_TILES
-CHUNKS = UNITS // UNITS_PER_CHUNK
-CHUNK_BUFS = 3
+FIRST_USE = -2
+INPUT_BUFS = 6
 
 FLOPS = 2 * TOKENS * A * D + 2 * TOKENS * D * F
 
@@ -35,36 +33,27 @@ def tile_swidtblock_pb_t_kernel(
     tc, attn_out, residual, wo, bo, ln2_gain, ln2_bias, w1, b1, out_0, out_1
 ):
     nc = tc.nc
-    attn_chunks = attn_out.flatten_outer_dims().rearrange("(c p i) k -> c p (i k)", p=P, i=CHUNK_TILES)
-    res_chunks = residual.flatten_outer_dims().rearrange("(c p i) d -> c p i d", p=P, i=CHUNK_TILES)
-    x_chunks = out_0.flatten_outer_dims().rearrange("(c p i) d -> c p i d", p=P, i=CHUNK_TILES)
-    g_chunks = out_1.flatten_outer_dims().rearrange("(c p i) f -> c p i f", p=P, i=CHUNK_TILES)
+    attn_units = attn_out.flatten_outer_dims().rearrange("(n p i) k -> n p (i k)", p=P, i=UNIT_TILES)
+    res_units = residual.flatten_outer_dims().rearrange("(n p i) d -> n p i d", p=P, i=UNIT_TILES)
+    x_units = out_0.flatten_outer_dims().rearrange("(n p i) d -> n p i d", p=P, i=UNIT_TILES)
+    g_units = out_1.flatten_outer_dims().rearrange("(n p i) f -> n p i f", p=P, i=UNIT_TILES)
 
     with ExitStack() as ctx:
         const = ctx.enter_context(tc.tile_pool(name="const", bufs=1))
-        chunks = ctx.enter_context(tc.tile_pool(name="chunks", bufs=CHUNK_BUFS))
+        inputs = ctx.enter_context(tc.tile_pool(name="inputs", bufs=INPUT_BUFS))
         work = ctx.enter_context(tc.tile_pool(name="work", bufs=2))
         held = ctx.enter_context(tc.tile_pool(name="held", bufs=3))
         psum = ctx.enter_context(tc.psum_pool(name="psum", bufs=2))
 
-        attn_of = {}
-        res_of = {}
+        live = {}
 
-        def load_chunk(c):
-            attn_sb = chunks.tile([P, CHUNK_TILES * A], BF16)
-            nc.sync.dma_start(out=attn_sb[:], in_=attn_chunks[c])
-            res_sb = chunks.tile([P, CHUNK_TILES, D], BF16)
-            nc.sync.dma_start(out=res_sb[:], in_=res_chunks[c])
-            attn_of[c] = attn_sb[:].bitcast(F32)
-            res_of[c] = res_sb
-
-        wo_raw = const.tile([P, PASSES, PACK, D], BF16)
-        wo_rows = wo.rearrange("(s u p e) c -> s p u (e c)", s=PASSES, u=2, p=P, e=2)
-        nc.sync.dma_start(out=wo_raw[:, 0].rearrange("p (u e) c -> p u (e c)", e=2), in_=wo_rows[0])
-        load_chunk(0)
-        nc.sync.dma_start(out=wo_raw[:, 1].rearrange("p (u e) c -> p u (e c)", e=2), in_=wo_rows[1])
-        load_chunk(1)
-        load_chunk(2)
+        def load(u):
+            attn_sb = inputs.tile([P, UNIT_TILES * A], BF16)
+            nc.sync.dma_start(out=attn_sb[:], in_=attn_units[u])
+            res_sb = inputs.tile([P, UNIT_TILES, D], BF16)
+            nc.sync.dma_start(out=res_sb[:], in_=res_units[u])
+            live["attn_words", u] = attn_sb[:].bitcast(F32)
+            live["res", u] = res_sb
 
         bias_rows = const.tile([P, D + F], BF16)
         nc.vector.memset(bias_rows[:], 0.0)
@@ -77,6 +66,13 @@ def tile_swidtblock_pb_t_kernel(
         w1_raw = const.tile([P, PACK, F], BF16)
         nc.scalar.dma_start(out=w1_raw[:], in_=w1.rearrange("(t p) f -> p t f", p=P))
 
+        wo_raw = const.tile([P, PASSES, PACK, D], BF16)
+        wo_rows = wo.rearrange("(s u p e) c -> s p u (e c)", s=PASSES, u=2, p=P, e=2)
+        for s in range(PASSES):
+            nc.sync.dma_start(out=wo_raw[:, s].rearrange("p (u e) c -> p u (e c)", e=2), in_=wo_rows[s])
+        for u in range(INPUT_BUFS):
+            load(u)
+
         ident_f32 = const.tile([P, P], F32)
         make_identity(nc, ident_f32[:])
         ident_bf16 = const.tile([P, P], BF16)
@@ -85,6 +81,8 @@ def tile_swidtblock_pb_t_kernel(
         nc.vector.memset(ones[:], 1.0)
         minus_half = const.tile([P, UNIT_TILES], F32)
         nc.vector.memset(minus_half[:], -0.5)
+        eps_col = const.tile([P, 1], F32)
+        nc.vector.memset(eps_col[:], EPS)
 
         wo_grouped = const.tile([P, PASSES, D * PACK], BF16, align_bytes=64)
         wo_codes = const.tile([P, PASSES, D], U32, align_bytes=64)
@@ -119,18 +117,12 @@ def tile_swidtblock_pb_t_kernel(
         norm_cols = const.tile([P, 2 * PACK], F32)
         nc.scalar.copy(out=norm_cols[:], in_=norm_ps[:, 0 : 2 * PACK])
 
-        live = {}
-
-        def chunk_and_first_tile(u):
-            return u // UNITS_PER_CHUNK, (u % UNITS_PER_CHUNK) * UNIT_TILES
-
         def transpose_attn(u):
-            c, first = chunk_and_first_tile(u)
             for i in range(UNIT_TILES):
                 at = psum.tile([P, PASSES * 2, P], F32, tag="at")
                 for w in range(PASSES * 2):
-                    start = (first + i) * (A // 2) + w * P
-                    nc.tensor.transpose(at[:, w, :], attn_of[c][:, start : start + P], ident_f32[:])
+                    start = i * (A // 2) + w * P
+                    nc.tensor.transpose(at[:, w, :], live["attn_words", u][:, start : start + P], ident_f32[:])
                 live["at", u, i] = at
 
         def group_attn(u):
@@ -171,18 +163,16 @@ def tile_swidtblock_pb_t_kernel(
                 live["acc", u, i] = acc
 
         def add_bias_to_residual(u):
-            c, first = chunk_and_first_tile(u)
             res_bo = held.tile([P, UNIT_TILES, D], F32)
             nc.vector.tensor_tensor(
                 out=res_bo[:],
-                in0=res_of[c][:, first : first + UNIT_TILES, :],
+                in0=live["res", u][:],
                 in1=bo_all[:].unsqueeze(1).to_broadcast([P, UNIT_TILES, D]),
                 op=ALU.add,
             )
             live["res_bo", u] = res_bo
 
         def finish_x_mid(u):
-            c, first = chunk_and_first_tile(u)
             x_mid = held.tile([P, UNIT_TILES, D], F32)
             row_sum = held.tile([P, UNIT_TILES], F32)
             for i in range(UNIT_TILES):
@@ -195,7 +185,7 @@ def tile_swidtblock_pb_t_kernel(
                     op1=ALU.add,
                     accum_out=row_sum[:, i : i + 1],
                 )
-            nc.sync.dma_start(out=x_chunks[c][:, first : first + UNIT_TILES, :], in_=x_mid[:])
+            nc.sync.dma_start(out=x_units[u], in_=x_mid[:])
             live["x_mid", u] = x_mid
             live["row_sum", u] = row_sum
 
@@ -214,9 +204,7 @@ def tile_swidtblock_pb_t_kernel(
                     accum_out=sq_sum[:, i : i + 1],
                 )
             var_eps = held.tile([P, UNIT_TILES], F32)
-            nc.gpsimd.tensor_scalar(
-                out=var_eps[:], in0=sq_sum[:], scalar1=1.0 / D, scalar2=EPS, op0=ALU.mult, op1=ALU.add
-            )
+            nc.scalar.activation(out=var_eps[:], in_=sq_sum[:], func=ACT.Identity, scale=1.0 / D, bias=eps_col[:])
             rstd = held.tile([P, UNIT_TILES], F32)
             nc.gpsimd.tensor_tensor(out=rstd[:], in0=var_eps[:], in1=minus_half[:], op=ALU.pow)
             live["neg_mean", u] = neg_mean
@@ -224,15 +212,25 @@ def tile_swidtblock_pb_t_kernel(
 
         def normalise(u):
             normed = work.tile([P, UNIT_TILES, D], F32)
-            for i in range(UNIT_TILES):
-                nc.vector.tensor_scalar(
-                    out=normed[:, i, :],
-                    in0=live["x_mid", u][:, i, :],
-                    scalar1=live["neg_mean", u][:, i : i + 1],
-                    scalar2=live["rstd", u][:, i : i + 1],
-                    op0=ALU.add,
-                    op1=ALU.mult,
-                )
+            nc.vector.tensor_scalar(
+                out=normed[:, 0, :],
+                in0=live["x_mid", u][:, 0, :],
+                scalar1=live["neg_mean", u][:, 0:1],
+                scalar2=live["rstd", u][:, 0:1],
+                op0=ALU.add,
+                op1=ALU.mult,
+            )
+            shift = held.tile([P, 1], F32)
+            nc.scalar.activation(
+                out=shift[:], in_=live["neg_mean", u][:, 1:2], func=ACT.Identity, scale=live["rstd", u][:, 1:2]
+            )
+            nc.scalar.activation(
+                out=normed[:, 1, :],
+                in_=live["x_mid", u][:, 1, :],
+                func=ACT.Identity,
+                scale=live["rstd", u][:, 1:2],
+                bias=shift[:],
+            )
             live["normed", u] = normed
 
         def transpose_normed(u):
@@ -298,32 +296,30 @@ def tile_swidtblock_pb_t_kernel(
             live["pre_gelu", u] = pre_gelu
 
         def gelu_and_store(u):
-            c, first = chunk_and_first_tile(u)
             g_sb = held.tile([P, UNIT_TILES, F], F32)
             nc.scalar.activation(out=g_sb[:], in_=live["pre_gelu", u][:], func=ACT.Gelu_apprx_tanh)
-            nc.sync.dma_start(out=g_chunks[c][:, first : first + UNIT_TILES, :], in_=g_sb[:])
+            nc.sync.dma_start(out=g_units[u], in_=g_sb[:])
 
         def when_valid(stage, u):
             if 0 <= u < UNITS:
                 stage(u)
 
-        for slot in range(-2, UNITS + 2):
-            if slot % UNITS_PER_CHUNK == 0:
-                next_chunk = slot // UNITS_PER_CHUNK + CHUNK_BUFS
-                if CHUNK_BUFS <= next_chunk < CHUNKS:
-                    load_chunk(next_chunk)
-            when_valid(transpose_normed, slot - 1)
-            when_valid(transpose_attn, slot + 2)
-            when_valid(finish_x_mid, slot)
-            when_valid(gain_and_bias, slot - 1)
-            when_valid(quantise_attn, slot + 1)
-            when_valid(project, slot + 1)
-            when_valid(statistics, slot)
-            when_valid(group_h, slot - 1)
-            when_valid(add_bias_to_residual, slot + 2)
-            when_valid(quantise_h, slot - 1)
-            when_valid(expand, slot - 1)
-            when_valid(gelu_and_store, slot - 2)
-            when_valid(group_attn, slot + 2)
-            when_valid(normalise, slot)
-            when_valid(add_b1, slot - 1)
+        with tc.manual_schedule():
+            for slot in range(FIRST_USE, UNITS + 3):
+                if slot > FIRST_USE:
+                    when_valid(load, slot - 1 - FIRST_USE + INPUT_BUFS)
+                when_valid(transpose_attn, slot + 2)
+                when_valid(finish_x_mid, slot)
+                when_valid(group_attn, slot + 2)
+                when_valid(group_h, slot - 2)
+                when_valid(normalise, slot - 1)
+                when_valid(transpose_normed, slot - 1)
+                when_valid(quantise_h, slot - 2)
+                when_valid(expand, slot - 2)
+                when_valid(quantise_attn, slot + 1)
+                when_valid(project, slot + 1)
+                when_valid(statistics, slot)
+                when_valid(gain_and_bias, slot - 1)
+                when_valid(add_bias_to_residual, slot + 2)
+                when_valid(add_b1, slot - 2)
+                when_valid(gelu_and_store, slot - 3)

@@ -23,8 +23,8 @@ PASSES = A // K_PASS
 UNIT_TILES = 2
 UNIT_TOKENS = UNIT_TILES * P
 UNITS = TOKENS // UNIT_TOKENS
-FIRST_USE = -2
 INPUT_BUFS = 6
+RUN = 4
 
 FLOPS = 2 * TOKENS * A * D + 2 * TOKENS * D * F
 
@@ -68,9 +68,10 @@ def tile_swidtblock_pb_t_kernel(
 
         wo_raw = const.tile([P, PASSES, PACK, D], BF16)
         wo_rows = wo.rearrange("(s u p e) c -> s p u (e c)", s=PASSES, u=2, p=P, e=2)
+        load(0)
         for s in range(PASSES):
             nc.sync.dma_start(out=wo_raw[:, s].rearrange("p (u e) c -> p u (e c)", e=2), in_=wo_rows[s])
-        for u in range(INPUT_BUFS):
+        for u in range(1, INPUT_BUFS):
             load(u)
 
         ident_f32 = const.tile([P, P], F32)
@@ -84,14 +85,17 @@ def tile_swidtblock_pb_t_kernel(
         eps_col = const.tile([P, 1], F32)
         nc.vector.memset(eps_col[:], EPS)
 
+        def regroup(copy, grouped, planes):
+            copy(
+                out=grouped.rearrange("p (c i t) -> p c t i", i=RUN, t=PACK),
+                in_=planes.rearrange("p t (c i) -> p c t i", i=RUN),
+            )
+
         wo_grouped = const.tile([P, PASSES, D * PACK], BF16, align_bytes=64)
         wo_codes = const.tile([P, PASSES, D], U32, align_bytes=64)
         wo_scales = const.tile([P, PASSES, D], U8, align_bytes=64)
-        for s in range(PASSES):
-            nc.vector.tensor_copy(
-                out=wo_grouped[:, s, :].rearrange("p (c t) -> p c t", t=PACK),
-                in_=wo_raw[:, s].rearrange("p t c -> p c t"),
-            )
+        regroup(nc.vector.tensor_copy, wo_grouped[:, 0, :], wo_raw[:, 0])
+        regroup(nc.scalar.copy, wo_grouped[:, 1, :], wo_raw[:, 1])
         for s in range(PASSES):
             nc.vector.quantize_mx(
                 out=wo_codes[:, s, :].bitcast(FP8X4), scales=wo_scales[:, s, :], in_=wo_grouped[:, s, :]
@@ -99,9 +103,7 @@ def tile_swidtblock_pb_t_kernel(
         w1_grouped = const.tile([P, F * PACK], BF16, align_bytes=64)
         w1_codes = const.tile([P, F], U32, align_bytes=64)
         w1_scales = const.tile([P, F], U8, align_bytes=64)
-        nc.scalar.copy(
-            out=w1_grouped[:].rearrange("p (f t) -> p f t", t=PACK), in_=w1_raw[:].rearrange("p t f -> p f t")
-        )
+        regroup(nc.scalar.copy, w1_grouped[:], w1_raw[:])
         nc.vector.quantize_mx(out=w1_codes[:].bitcast(FP8X4), scales=w1_scales[:], in_=w1_grouped[:])
 
         bo_ps = psum.tile([P, D], F32, tag="acc")
@@ -189,9 +191,12 @@ def tile_swidtblock_pb_t_kernel(
             live["x_mid", u] = x_mid
             live["row_sum", u] = row_sum
 
-        def statistics(u):
+        def negate_mean(u):
             neg_mean = held.tile([P, UNIT_TILES], F32)
             nc.scalar.mul(out=neg_mean[:], in_=live["row_sum", u][:], mul=-1.0 / D)
+            live["neg_mean", u] = neg_mean
+
+        def sum_squares(u):
             sq_sum = held.tile([P, UNIT_TILES], F32)
             for i in range(UNIT_TILES):
                 squares = work.tile([P, D], BF16)
@@ -199,18 +204,22 @@ def tile_swidtblock_pb_t_kernel(
                     out=squares[:],
                     in_=live["x_mid", u][:, i, :],
                     func=ACT.Square,
-                    bias=neg_mean[:, i : i + 1],
+                    bias=live["neg_mean", u][:, i : i + 1],
                     scale=1.0,
                     accum_out=sq_sum[:, i : i + 1],
                 )
+            live["sq_sum", u] = sq_sum
+
+        def inverse_std(u):
             var_eps = held.tile([P, UNIT_TILES], F32)
-            nc.scalar.activation(out=var_eps[:], in_=sq_sum[:], func=ACT.Identity, scale=1.0 / D, bias=eps_col[:])
+            nc.scalar.activation(
+                out=var_eps[:], in_=live["sq_sum", u][:], func=ACT.Identity, scale=1.0 / D, bias=eps_col[:]
+            )
             rstd = held.tile([P, UNIT_TILES], F32)
             nc.gpsimd.tensor_tensor(out=rstd[:], in0=var_eps[:], in1=minus_half[:], op=ALU.pow)
-            live["neg_mean", u] = neg_mean
             live["rstd", u] = rstd
 
-        def normalise(u):
+        def normalise_tile_0(u):
             normed = work.tile([P, UNIT_TILES, D], F32)
             nc.vector.tensor_scalar(
                 out=normed[:, 0, :],
@@ -220,18 +229,23 @@ def tile_swidtblock_pb_t_kernel(
                 op0=ALU.add,
                 op1=ALU.mult,
             )
+            live["normed", u] = normed
+
+        def shift_of_tile_1(u):
             shift = held.tile([P, 1], F32)
             nc.scalar.activation(
                 out=shift[:], in_=live["neg_mean", u][:, 1:2], func=ACT.Identity, scale=live["rstd", u][:, 1:2]
             )
+            live["shift", u] = shift
+
+        def normalise_tile_1(u):
             nc.scalar.activation(
-                out=normed[:, 1, :],
+                out=live["normed", u][:, 1, :],
                 in_=live["x_mid", u][:, 1, :],
                 func=ACT.Identity,
                 scale=live["rstd", u][:, 1:2],
-                bias=shift[:],
+                bias=live["shift", u][:],
             )
-            live["normed", u] = normed
 
         def transpose_normed(u):
             for half in range(2):
@@ -258,10 +272,7 @@ def tile_swidtblock_pb_t_kernel(
 
         def group_h(u):
             h_grouped = work.tile([P, UNIT_TOKENS * PACK], BF16, align_bytes=64)
-            nc.vector.tensor_copy(
-                out=h_grouped[:].rearrange("p (j t) -> p j t", t=PACK),
-                in_=live["h_planes", u][:].rearrange("p t j -> p j t"),
-            )
+            regroup(nc.vector.tensor_copy, h_grouped[:], live["h_planes", u][:])
             live["h_grouped", u] = h_grouped
 
         def quantise_h(u):
@@ -305,21 +316,25 @@ def tile_swidtblock_pb_t_kernel(
                 stage(u)
 
         with tc.manual_schedule():
-            for slot in range(FIRST_USE, UNITS + 3):
-                if slot > FIRST_USE:
-                    when_valid(load, slot - 1 - FIRST_USE + INPUT_BUFS)
+            for slot in range(-2, UNITS + 7):
+                if slot >= 0:
+                    when_valid(load, slot + INPUT_BUFS)
+                when_valid(project, slot)
+                when_valid(expand, slot - 5)
+                when_valid(transpose_normed, slot - 3)
                 when_valid(transpose_attn, slot + 2)
-                when_valid(finish_x_mid, slot)
-                when_valid(group_attn, slot + 2)
-                when_valid(group_h, slot - 2)
-                when_valid(normalise, slot - 1)
-                when_valid(transpose_normed, slot - 1)
-                when_valid(quantise_h, slot - 2)
-                when_valid(expand, slot - 2)
                 when_valid(quantise_attn, slot + 1)
-                when_valid(project, slot + 1)
-                when_valid(statistics, slot)
-                when_valid(gain_and_bias, slot - 1)
-                when_valid(add_bias_to_residual, slot + 2)
-                when_valid(add_b1, slot - 2)
-                when_valid(gelu_and_store, slot - 3)
+                when_valid(normalise_tile_0, slot - 2)
+                when_valid(group_h, slot - 4)
+                when_valid(add_bias_to_residual, slot + 1)
+                when_valid(quantise_h, slot - 4)
+                when_valid(finish_x_mid, slot)
+                when_valid(add_b1, slot - 5)
+                when_valid(negate_mean, slot - 1)
+                when_valid(shift_of_tile_1, slot - 2)
+                when_valid(gelu_and_store, slot - 6)
+                when_valid(sum_squares, slot - 1)
+                when_valid(normalise_tile_1, slot - 2)
+                when_valid(inverse_std, slot - 1)
+                when_valid(gain_and_bias, slot - 3)
+                when_valid(group_attn, slot + 2)

@@ -68,10 +68,9 @@ def tile_swidtblock_pb_t_kernel(
 
         wo_raw = const.tile([P, PASSES, PACK, D], BF16)
         wo_rows = wo.rearrange("(s u p e) c -> s p u (e c)", s=PASSES, u=2, p=P, e=2)
-        load(0)
         for s in range(PASSES):
             nc.sync.dma_start(out=wo_raw[:, s].rearrange("p (u e) c -> p u (e c)", e=2), in_=wo_rows[s])
-        for u in range(1, INPUT_BUFS):
+        for u in range(INPUT_BUFS):
             load(u)
 
         ident_f32 = const.tile([P, P], F32)
@@ -94,8 +93,8 @@ def tile_swidtblock_pb_t_kernel(
         wo_grouped = const.tile([P, PASSES, D * PACK], BF16, align_bytes=64)
         wo_codes = const.tile([P, PASSES, D], U32, align_bytes=64)
         wo_scales = const.tile([P, PASSES, D], U8, align_bytes=64)
-        regroup(nc.vector.tensor_copy, wo_grouped[:, 0, :], wo_raw[:, 0])
-        regroup(nc.scalar.copy, wo_grouped[:, 1, :], wo_raw[:, 1])
+        for s in range(PASSES):
+            regroup(nc.vector.tensor_copy, wo_grouped[:, s, :], wo_raw[:, s])
         for s in range(PASSES):
             nc.vector.quantize_mx(
                 out=wo_codes[:, s, :].bitcast(FP8X4), scales=wo_scales[:, s, :], in_=wo_grouped[:, s, :]
@@ -323,11 +322,11 @@ def tile_swidtblock_pb_t_kernel(
                 when_valid(expand, slot - 5)
                 when_valid(transpose_normed, slot - 3)
                 when_valid(transpose_attn, slot + 2)
-                when_valid(quantise_attn, slot + 1)
                 when_valid(normalise_tile_0, slot - 2)
                 when_valid(group_h, slot - 4)
                 when_valid(add_bias_to_residual, slot + 1)
                 when_valid(quantise_h, slot - 4)
+                when_valid(quantise_attn, slot + 1)
                 when_valid(finish_x_mid, slot)
                 when_valid(add_b1, slot - 5)
                 when_valid(negate_mean, slot - 1)

@@ -314,26 +314,25 @@ def tile_swidtblock_pb_t_kernel(
             if 0 <= u < UNITS:
                 stage(u)
 
-        with tc.manual_schedule():
-            for slot in range(-2, UNITS + 7):
-                if slot >= 0:
-                    when_valid(load, slot + INPUT_BUFS)
-                when_valid(project, slot)
-                when_valid(expand, slot - 5)
-                when_valid(transpose_normed, slot - 3)
-                when_valid(transpose_attn, slot + 2)
-                when_valid(normalise_tile_0, slot - 2)
-                when_valid(group_h, slot - 4)
-                when_valid(add_bias_to_residual, slot + 1)
-                when_valid(quantise_h, slot - 4)
-                when_valid(quantise_attn, slot + 1)
-                when_valid(finish_x_mid, slot)
-                when_valid(add_b1, slot - 5)
-                when_valid(negate_mean, slot - 1)
-                when_valid(shift_of_tile_1, slot - 2)
-                when_valid(gelu_and_store, slot - 6)
-                when_valid(sum_squares, slot - 1)
-                when_valid(normalise_tile_1, slot - 2)
-                when_valid(inverse_std, slot - 1)
-                when_valid(gain_and_bias, slot - 3)
-                when_valid(group_attn, slot + 2)
+        for slot in range(-2, UNITS + 7):
+            if slot >= 0:
+                when_valid(load, slot + INPUT_BUFS)
+            when_valid(project, slot)
+            when_valid(expand, slot - 5)
+            when_valid(transpose_normed, slot - 3)
+            when_valid(transpose_attn, slot + 2)
+            when_valid(normalise_tile_0, slot - 2)
+            when_valid(group_h, slot - 4)
+            when_valid(add_bias_to_residual, slot + 1)
+            when_valid(quantise_h, slot - 4)
+            when_valid(quantise_attn, slot + 1)
+            when_valid(finish_x_mid, slot)
+            when_valid(add_b1, slot - 5)
+            when_valid(negate_mean, slot - 1)
+            when_valid(shift_of_tile_1, slot - 2)
+            when_valid(gelu_and_store, slot - 6)
+            when_valid(sum_squares, slot - 1)
+            when_valid(normalise_tile_1, slot - 2)
+            when_valid(inverse_std, slot - 1)
+            when_valid(gain_and_bias, slot - 3)
+            when_valid(group_attn, slot + 2)

from contextlib import ExitStack

import concourse.mybir as mybir
from concourse.masks import make_identity

F32 = mybir.dt.float32
BF16 = mybir.dt.bfloat16
U32 = mybir.dt.uint32
U8 = mybir.dt.uint8
FP8X4 = mybir.dt.float8_e4m3fn_x4
ALU = mybir.AluOpType
ACT = mybir.ActivationFunctionType

P = 128
PACK = 4
K_PASS = P * PACK
TOKENS = 4 * 1024
A = 1024
D = 512
F = 256
EPS = 1e-6
PASSES = A // K_PASS
UNIT_TILES = 2
UNIT_TOKENS = UNIT_TILES * P
UNITS = TOKENS // UNIT_TOKENS
INPUT_BUFS = 6
RUN = 4

FLOPS = 2 * TOKENS * A * D + 2 * TOKENS * D * F


def tile_swidtblock_pb_t_kernel(
    tc, attn_out, residual, wo, bo, ln2_gain, ln2_bias, w1, b1, out_0, out_1
):
    nc = tc.nc
    attn_units = attn_out.flatten_outer_dims().rearrange("(n p i) k -> n p (i k)", p=P, i=UNIT_TILES)
    res_units = residual.flatten_outer_dims().rearrange("(n p i) d -> n p i d", p=P, i=UNIT_TILES)
    x_units = out_0.flatten_outer_dims().rearrange("(n p i) d -> n p i d", p=P, i=UNIT_TILES)
    g_units = out_1.flatten_outer_dims().rearrange("(n p i) f -> n p i f", p=P, i=UNIT_TILES)

    with ExitStack() as ctx:
        const = ctx.enter_context(tc.tile_pool(name="const", bufs=1))
        inputs = ctx.enter_context(tc.tile_pool(name="inputs", bufs=INPUT_BUFS))
        work = ctx.enter_context(tc.tile_pool(name="work", bufs=2))
        held = ctx.enter_context(tc.tile_pool(name="held", bufs=3))
        psum = ctx.enter_context(tc.psum_pool(name="psum", bufs=2))

        live = {}

        def load(u):
            attn_sb = inputs.tile([P, UNIT_TILES * A], BF16)
            nc.sync.dma_start(out=attn_sb[:], in_=attn_units[u])
            res_sb = inputs.tile([P, UNIT_TILES, D], BF16)
            nc.sync.dma_start(out=res_sb[:], in_=res_units[u])
            live["attn_words", u] = attn_sb[:].bitcast(F32)
            live["res", u] = res_sb

        bias_rows = const.tile([P, D + F], BF16)
        nc.vector.memset(bias_rows[:], 0.0)
        nc.scalar.dma_start(out=bias_rows[0:1, 0:D], in_=bo.rearrange("(o d) -> o d", o=1))
        nc.scalar.dma_start(out=bias_rows[0:1, D : D + F], in_=b1.rearrange("(o f) -> o f", o=1))
        norm_rows = const.tile([P, P], BF16)
        nc.vector.memset(norm_rows[:], 0.0)
        nc.scalar.dma_start(out=norm_rows[0:PACK, :], in_=ln2_gain.rearrange("(t p) -> t p", p=P))
        nc.scalar.dma_start(out=norm_rows[PACK : 2 * PACK, :], in_=ln2_bias.rearrange("(t p) -> t p", p=P))
        w1_raw = const.tile([P, PACK, F], BF16)
        nc.scalar.dma_start(out=w1_raw[:], in_=w1.rearrange("(t p) f -> p t f", p=P))

        wo_raw = const.tile([P, PASSES, PACK, D], BF16)
        wo_rows = wo.rearrange("(s u p e) c -> s p u (e c)", s=PASSES, u=2, p=P, e=2)
        for s in range(PASSES):
            nc.sync.dma_start(out=wo_raw[:, s].rearrange("p (u e) c -> p u (e c)", e=2), in_=wo_rows[s])
        for u in range(INPUT_BUFS):
            load(u)

        ident_f32 = const.tile([P, P], F32)
        make_identity(nc, ident_f32[:])
        ident_bf16 = const.tile([P, P], BF16)
        make_identity(nc, ident_bf16[:])
        ones = const.tile([P, P], BF16)
        nc.vector.memset(ones[:], 1.0)
        minus_half = const.tile([P, UNIT_TILES], F32)
        nc.vector.memset(minus_half[:], -0.5)
        eps_col = const.tile([P, 1], F32)
        nc.vector.memset(eps_col[:], EPS)

        def regroup(copy, grouped, planes):
            copy(
                out=grouped.rearrange("p (c i t) -> p c t i", i=RUN, t=PACK),
                in_=planes.rearrange("p t (c i) -> p c t i", i=RUN),
            )

        wo_grouped = const.tile([P, PASSES, D * PACK], BF16, align_bytes=64)
        wo_codes = const.tile([P, PASSES, D], U32, align_bytes=64)
        wo_scales = const.tile([P, PASSES, D], U8, align_bytes=64)
        for s in range(PASSES):
            regroup(nc.vector.tensor_copy, wo_grouped[:, s, :], wo_raw[:, s])
        for s in range(PASSES):
            nc.vector.quantize_mx(
                out=wo_codes[:, s, :].bitcast(FP8X4), scales=wo_scales[:, s, :], in_=wo_grouped[:, s, :]
            )
        w1_grouped = const.tile([P, F * PACK], BF16, align_bytes=64)
        w1_codes = const.tile([P, F], U32, align_bytes=64)
        w1_scales = const.tile([P, F], U8, align_bytes=64)
        regroup(nc.scalar.copy, w1_grouped[:], w1_raw[:])
        nc.vector.quantize_mx(out=w1_codes[:].bitcast(FP8X4), scales=w1_scales[:], in_=w1_grouped[:])

        bo_ps = psum.tile([P, D], F32, tag="acc")
        nc.tensor.matmul(out=bo_ps[:], lhsT=ones[:], rhs=bias_rows[:, 0:D], start=True, stop=True)
        bo_all = const.tile([P, D], F32)
        nc.scalar.copy(out=bo_all[:], in_=bo_ps[:])
        b1_ps = psum.tile([P, F], F32, tag="acc")
        nc.tensor.matmul(out=b1_ps[:], lhsT=ones[:], rhs=bias_rows[:, D : D + F], start=True, stop=True)
        b1_all = const.tile([P, F], F32)
        nc.scalar.copy(out=b1_all[:], in_=b1_ps[:])
        norm_ps = psum.tile([P, P], BF16, tag="at")
        nc.tensor.transpose(norm_ps[:], norm_rows[:], ident_bf16[:])
        norm_cols = const.tile([P, 2 * PACK], F32)
        nc.scalar.copy(out=norm_cols[:], in_=norm_ps[:, 0 : 2 * PACK])

        def transpose_attn(u):
            for i in range(UNIT_TILES):
                at = psum.tile([P, PASSES * 2, P], F32, tag="at")
                for w in range(PASSES * 2):
                    start = i * (A // 2) + w * P
                    nc.tensor.transpose(at[:, w, :], live["attn_words", u][:, start : start + P], ident_f32[:])
                live["at", u, i] = at

        def group_attn(u):
            a_grouped = work.tile([P, UNIT_TILES * PASSES * P * PACK], BF16, align_bytes=64)
            words = a_grouped[:].bitcast(F32).rearrange(
                "p (i s j u) -> p i s j u", i=UNIT_TILES, s=PASSES, u=2
            )
            for i in range(UNIT_TILES):
                nc.scalar.copy(
                    out=words[:, i], in_=live["at", u, i][:].rearrange("p (s u) j -> p s j u", u=2)
                )
            live["a_grouped", u] = a_grouped

        def quantise_attn(u):
            a_codes = work.tile([P, UNIT_TILES, PASSES, P], U32, align_bytes=64)
            a_scales = work.tile([P, UNIT_TILES, PASSES, P], U8, align_bytes=64)
            nc.vector.quantize_mx(
                out=a_codes[:].rearrange("p i s j -> p (i s j)").bitcast(FP8X4),
                scales=a_scales[:].rearrange("p i s j -> p (i s j)"),
                in_=live["a_grouped", u][:],
            )
            live["a_codes", u] = a_codes
            live["a_scales", u] = a_scales

        def project(u):
            for i in range(UNIT_TILES):
                acc = psum.tile([P, D], F32, tag="acc")
                for s in range(PASSES):
                    nc.tensor.matmul_mx(
                        out=acc[:],
                        lhsT=live["a_codes", u][:, i, s, :].bitcast(FP8X4),
                        lhsT_scale=live["a_scales", u][:, i, s, :],
                        rhs=wo_codes[:, s, :].bitcast(FP8X4),
                        rhs_scale=wo_scales[:, s, :],
                        start=(s == 0),
                        stop=(s == PASSES - 1),
                    )
                live["acc", u, i] = acc

        def add_bias_to_residual(u):
            res_bo = held.tile([P, UNIT_TILES, D], F32)
            nc.vector.tensor_tensor(
                out=res_bo[:],
                in0=live["res", u][:],
                in1=bo_all[:].unsqueeze(1).to_broadcast([P, UNIT_TILES, D]),
                op=ALU.add,
            )
            live["res_bo", u] = res_bo

        def finish_x_mid(u):
            x_mid = held.tile([P, UNIT_TILES, D], F32)
            row_sum = held.tile([P, UNIT_TILES], F32)
            for i in range(UNIT_TILES):
                nc.vector.scalar_tensor_tensor(
                    out=x_mid[:, i, :],
                    in0=live["acc", u, i][:],
                    scalar=0.0,
                    in1=live["res_bo", u][:, i, :],
                    op0=ALU.add,
                    op1=ALU.add,
                    accum_out=row_sum[:, i : i + 1],
                )
            nc.sync.dma_start(out=x_units[u], in_=x_mid[:])
            live["x_mid", u] = x_mid
            live["row_sum", u] = row_sum

        def negate_mean(u):
            neg_mean = held.tile([P, UNIT_TILES], F32)
            nc.scalar.mul(out=neg_mean[:], in_=live["row_sum", u][:], mul=-1.0 / D)
            live["neg_mean", u] = neg_mean

        def sum_squares(u):
            sq_sum = held.tile([P, UNIT_TILES], F32)
            for i in range(UNIT_TILES):
                squares = work.tile([P, D], BF16)
                nc.scalar.activation(
                    out=squares[:],
                    in_=live["x_mid", u][:, i, :],
                    func=ACT.Square,
                    bias=live["neg_mean", u][:, i : i + 1],
                    scale=1.0,
                    accum_out=sq_sum[:, i : i + 1],
                )
            live["sq_sum", u] = sq_sum

        def inverse_std(u):
            var_eps = held.tile([P, UNIT_TILES], F32)
            nc.scalar.activation(
                out=var_eps[:], in_=live["sq_sum", u][:], func=ACT.Identity, scale=1.0 / D, bias=eps_col[:]
            )
            rstd = held.tile([P, UNIT_TILES], F32)
            nc.gpsimd.tensor_tensor(out=rstd[:], in0=var_eps[:], in1=minus_half[:], op=ALU.pow)
            live["rstd", u] = rstd

        def normalise_tile_0(u):
            normed = work.tile([P, UNIT_TILES, D], F32)
            nc.vector.tensor_scalar(
                out=normed[:, 0, :],
                in0=live["x_mid", u][:, 0, :],
                scalar1=live["neg_mean", u][:, 0:1],
                scalar2=live["rstd", u][:, 0:1],
                op0=ALU.add,
                op1=ALU.mult,
            )
            live["normed", u] = normed

        def shift_of_tile_1(u):
            shift = held.tile([P, 1], F32)
            nc.scalar.activation(
                out=shift[:], in_=live["neg_mean", u][:, 1:2], func=ACT.Identity, scale=live["rstd", u][:, 1:2]
            )
            live["shift", u] = shift

        def normalise_tile_1(u):
            nc.scalar.activation(
                out=live["normed", u][:, 1, :],
                in_=live["x_mid", u][:, 1, :],
                func=ACT.Identity,
                scale=live["rstd", u][:, 1:2],
                bias=live["shift", u][:],
            )

        def transpose_normed(u):
            for half in range(2):
                planes = psum.tile([P, PACK // 2, UNIT_TILES, P], F32, tag="planes")
                for t2 in range(PACK // 2):
                    t = half * (PACK // 2) + t2
                    for i in range(UNIT_TILES):
                        nc.tensor.transpose(
                            planes[:, t2, i, :], live["normed", u][:, i, t * P : (t + 1) * P], ident_f32[:]
                        )
                live["planes", u, half] = planes

        def gain_and_bias(u):
            h_planes = work.tile([P, PACK, UNIT_TOKENS], BF16)
            for t in range(PACK):
                nc.scalar.activation(
                    out=h_planes[:, t, :],
                    in_=live["planes", u, t // (PACK // 2)][:, t % (PACK // 2)].rearrange("p i j -> p (i j)"),
                    func=ACT.Identity,
                    scale=norm_cols[:, t : t + 1],
                    bias=norm_cols[:, PACK + t : PACK + t + 1],
                )
            live["h_planes", u] = h_planes

        def group_h(u):
            h_grouped = work.tile([P, UNIT_TOKENS * PACK], BF16, align_bytes=64)
            regroup(nc.vector.tensor_copy, h_grouped[:], live["h_planes", u][:])
            live["h_grouped", u] = h_grouped

        def quantise_h(u):
            h_codes = work.tile([P, UNIT_TOKENS], U32, align_bytes=64)
            h_scales = work.tile([P, UNIT_TOKENS], U8, align_bytes=64)
            nc.vector.quantize_mx(out=h_codes[:].bitcast(FP8X4), scales=h_scales[:], in_=live["h_grouped", u][:])
            live["h_codes", u] = h_codes
            live["h_scales", u] = h_scales

        def expand(u):
            acc2 = psum.tile([P, UNIT_TILES, F], F32, tag="acc2")
            for i in range(UNIT_TILES):
                nc.tensor.matmul_mx(
                    out=acc2[:, i, :],
                    lhsT=live["h_codes", u][:, i * P : (i + 1) * P].bitcast(FP8X4),
                    lhsT_scale=live["h_scales", u][:, i * P : (i + 1) * P],
                    rhs=w1_codes[:].bitcast(FP8X4),
                    rhs_scale=w1_scales[:],
                    start=True,
                    stop=True,
                )
            live["acc2", u] = acc2

        def add_b1(u):
            pre_gelu = work.tile([P, UNIT_TILES, F], F32)
            nc.vector.tensor_tensor(
                out=pre_gelu[:],
                in0=live["acc2", u][:],
                in1=b1_all[:].unsqueeze(1).to_broadcast([P, UNIT_TILES, F]),
                op=ALU.add,
            )
            live["pre_gelu", u] = pre_gelu

        def gelu_and_store(u):
            g_sb = held.tile([P, UNIT_TILES, F], F32)
            nc.scalar.activation(out=g_sb[:], in_=live["pre_gelu", u][:], func=ACT.Gelu_apprx_tanh)
            nc.sync.dma_start(out=g_units[u], in_=g_sb[:])

        def when_valid(stage, u):
            if 0 <= u < UNITS:
                stage(u)

        for slot in range(-2, UNITS + 7):
            if slot >= 0:
                when_valid(load, slot + INPUT_BUFS)
            when_valid(project, slot)
            when_valid(expand, slot - 5)
            when_valid(transpose_normed, slot - 3)
            when_valid(transpose_attn, slot + 2)
            when_valid(normalise_tile_0, slot - 2)
            when_valid(group_h, slot - 4)
            when_valid(add_bias_to_residual, slot + 1)
            when_valid(quantise_h, slot - 4)
            when_valid(quantise_attn, slot + 1)
            when_valid(finish_x_mid, slot)
            when_valid(add_b1, slot - 5)
            when_valid(negate_mean, slot - 1)
            when_valid(shift_of_tile_1, slot - 2)
            when_valid(gelu_and_store, slot - 6)
            when_valid(sum_squares, slot - 1)
            when_valid(normalise_tile_1, slot - 2)
            when_valid(inverse_std, slot - 1)
            when_valid(gain_and_bias, slot - 3)
            when_valid(group_attn, slot + 2)
